import numpy as np
import ml_dtypes


def mxq(x, axis, fmt="e4m3"):
    dtype, down = {"e4m3": (ml_dtypes.float8_e4m3fn, 7), "e5m2": (ml_dtypes.float8_e5m2, 14)}[fmt]
    v = np.moveaxis(np.asarray(x, np.float32).astype(ml_dtypes.bfloat16).astype(np.float64), axis, -1)
    blocks = v.reshape(v.shape[:-1] + (-1, 32))
    amax = np.abs(blocks).max(-1, keepdims=True)
    byte = np.maximum(np.where(amax > 0, np.frexp(amax)[1] - 1 + 127, 0) - down, 1)
    scale = np.exp2(byte - 127.0)
    codes = (blocks / scale).astype(np.float32).astype(dtype).astype(np.float64)
    return np.moveaxis((codes * scale).reshape(v.shape), -1, axis)


WIDE = False


def mx_kscale(k):
    if not WIDE:
        return np.ones(k)
    levels = np.array([10, -10, 5, -5, 0])
    a = np.random.permutation(np.resize(levels, k // 512 * 4)).reshape(k // 512, 4)
    idx = np.arange(k)
    return np.exp2(a[idx // 512, idx % 128 // 32])


BF16 = ml_dtypes.bfloat16


def bf(x):
    return np.asarray(x, np.float32).astype(BF16)


def f64(x):
    return np.asarray(x).astype(np.float64)


E2M1 = np.array([0.0, 0.5, 1.0, 1.5, 2.0, 3.0, 4.0, 6.0, -0.0, -0.5, -1.0, -1.5, -2.0, -3.0, -4.0, -6.0])


def pack_weight(w, fmt):
    k, n = w.shape
    w = f64(bf(w)).reshape(k // 32, 32, n)
    amax = np.abs(w).max(1)
    if fmt == "e4m3":
        byte = np.frexp(amax)[1] - 1 + 127 - 7
    else:
        mant, ex = np.frexp(amax / 6.0)
        byte = np.where(mant > 0.5, ex, ex - 1) + 127
    byte = np.clip(np.where(amax > 0, byte, 1), 1, 254)
    scaled = (w * np.exp2(127.0 - byte)[:, None, :]).reshape(k, n).astype(np.float32)
    by_word = np.ascontiguousarray(scaled.reshape(k // 512, 128, 4, n).transpose(0, 1, 3, 2))
    if fmt == "e4m3":
        words = by_word.astype(ml_dtypes.float8_e4m3fn).view(np.uint8)
    else:
        c = by_word.astype(ml_dtypes.float4_e2m1fn).view(np.uint8) & 0xF
        words = c[..., 0::2] | (c[..., 1::2] << 4)
    return np.ascontiguousarray(words), np.ascontiguousarray(byte.astype(np.uint8).reshape(k // 512, 16, n))


def unpack_weight(words, scales, fmt):
    g, p, n, _ = words.shape
    if fmt == "e4m3":
        vals = np.ascontiguousarray(words).view(ml_dtypes.float8_e4m3fn).astype(np.float64)
    else:
        nib = np.empty((g, p, n, 4), np.uint8)
        nib[..., 0::2] = words & 0xF
        nib[..., 1::2] = words >> 4
        vals = E2M1[nib]
    vals = vals * np.repeat(np.exp2(scales.astype(np.float64) - 127.0), 8, axis=1)[..., None]
    return vals.transpose(0, 1, 3, 2).reshape(g * 512, n)


B, IN_C, OUT_C, HM, HN, NL = 256, 512, 512, 512, 16, 3


def leaky(v, leak):
    return np.where(v < 0, v * leak, v)


def setup_inputs():
    s = mx_kscale(IN_C)
    x = bf(np.random.standard_normal((B, IN_C)) * s)
    w_im = np.random.standard_normal((HN, IN_C, HM)) * 0.7 / np.sqrt(IN_C) / s[None, :, None]
    w_in = np.random.standard_normal((HM, IN_C, HN)) * 0.7 / np.sqrt(IN_C) / s[None, :, None]
    leak_m = bf(np.random.uniform(-2.0, 2.0, HM))
    leak_n = bf(np.random.uniform(-2.0, 2.0, HN))
    im_words, im_scales = pack_weight(w_im.reshape(-1, HM), "e4m3")
    in_words, in_scales = pack_weight(w_in.reshape(-1, HN), "e4m3")
    return {"x": x,
            "W_im_words": im_words, "W_im_scales": im_scales,
            "W_in_words": in_words, "W_in_scales": in_scales,
            "leak_m": leak_m,
            "leak_n": leak_n}


def reference(x, W_im_words, W_im_scales, W_in_words, W_in_scales, leak_m, leak_n):
    xq = mxq(f64(x), 1, "e4m3")
    wim = unpack_weight(W_im_words, W_im_scales, "e4m3").reshape(HN, IN_C, HM).transpose(1, 0, 2).reshape(IN_C, HN * HM)
    win = unpack_weight(W_in_words, W_in_scales, "e4m3").reshape(HM, IN_C, HN).transpose(1, 0, 2).reshape(IN_C, HM * HN)
    x_m = leaky((xq @ wim).reshape(B, HN, HM), f64(leak_m))
    x_n = leaky((xq @ win).reshape(B, HM, HN), f64(leak_n))
    return x_m + x_n.transpose(0, 2, 1)

@@ -1,0 +1,185 @@
+from contextlib import ExitStack
+
+import concourse.mybir as mybir
+from concourse.masks import make_identity
+
+F32 = mybir.dt.float32
+BF16 = mybir.dt.bfloat16
+I32 = mybir.dt.int32
+U32 = mybir.dt.uint32
+U8 = mybir.dt.uint8
+FP8X4 = mybir.dt.float8_e4m3fn_x4
+ALU = mybir.AluOpType
+ACT = mybir.ActivationFunctionType
+
+P = 128
+B, K, HM, HN = 256, 512, 512, 16
+B_TILES = B // P
+N_PASS = 512
+M_PER_PASS = N_PASS // HN
+GROUP_M = 128
+PASSES_PER_GROUP = GROUP_M // M_PER_PASS
+GROUPS = HM // GROUP_M
+EARLY_M = (GROUPS - 1) * GROUP_M
+
+FLOPS = 2 * B * K * (HN * HM) * 2
+
+
+def tile_tensormoe_pa_e_kernel(
+    tc, x, W_im_words, W_im_scales, W_in_words, W_in_scales, leak_m, leak_n, out
+):
+    nc = tc.nc
+    with ExitStack() as ctx:
+        keep = ctx.enter_context(tc.tile_pool(name="keep", bufs=1))
+        work = ctx.enter_context(tc.tile_pool(name="work", bufs=4))
+        parts = ctx.enter_context(tc.tile_pool(name="parts", bufs=3))
+
+        im_words = keep.tile([P, HN * HM], U32, align_bytes=64)
+        im_scales = keep.tile([P, HN * HM], U8, align_bytes=64)
+        in_words = keep.tile([P, HM * HN], U32, align_bytes=64)
+        in_scales = keep.tile([P, HM * HN], U8, align_bytes=64)
+        x_words = keep.tile([P, B], U32, align_bytes=64)
+        x_scales = keep.tile([P, B], U8, align_bytes=64)
+        slope_m = keep.tile([P, HM], F32)
+        minus_slope_n = keep.tile([P, HN], F32)
+        total = [keep.tile([P, HN, HM], F32, name="total%d" % t) for t in range(B_TILES)]
+
+        nc.vector.memset(im_scales[:].bitcast(I32), 0)
+        nc.vector.memset(in_scales[:].bitcast(I32), 0)
+
+        x_rows = keep.tile([P, B_TILES, K], BF16)
+        nc.sync.dma_start(out=x_rows[:], in_=x.rearrange("(t b) k -> b t k", b=P))
+        for quad in range(4):
+            nc.sync.dma_start(
+                out=im_scales[32 * quad : 32 * quad + 4, :]
+                .bitcast(I32)
+                .rearrange("r (g w) -> r g w", g=HN),
+                in_=W_im_scales[:, 4 * quad : 4 * quad + 4, :]
+                .rearrange("g r c -> r g c")
+                .bitcast(I32),
+            )
+        slopes_row = keep.tile([P, HM + 32], BF16)
+        nc.gpsimd.memset(slopes_row[:], 0.0)
+        nc.sync.dma_start(out=slopes_row[0:1, 0:HM], in_=leak_m.unsqueeze(0))
+        nc.sync.dma_start(out=slopes_row[0:1, HM : HM + HN], in_=leak_n.unsqueeze(0))
+        for j in range(4):
+            nc.sync.dma_start(
+                out=im_words[:, 4 * j * HM : 4 * (j + 1) * HM]
+                .bitcast(I32)
+                .rearrange("p (g w) -> p g w", g=4),
+                in_=W_im_words[4 * j : 4 * (j + 1)]
+                .rearrange("g p n t -> p g (n t)")
+                .bitcast(I32),
+            )
+        for q in range(16):
+            row = 32 * (q // 4) + q % 4
+            nc.sync.dma_start(
+                out=in_scales[row : row + 1, :].bitcast(I32).rearrange("o (m w) -> o m w", m=HM),
+                in_=W_in_scales[:, q, :].bitcast(I32).unsqueeze(0),
+            )
+        for c in range(HM // M_PER_PASS):
+            nc.sync.dma_start(
+                out=in_words[:, c * N_PASS : (c + 1) * N_PASS]
+                .bitcast(I32)
+                .rearrange("p (m w) -> p m w", m=M_PER_PASS),
+                in_=W_in_words[c * M_PER_PASS : (c + 1) * M_PER_PASS]
+                .rearrange("m p n t -> p m (n t)")
+                .bitcast(I32),
+            )
+
+        identity = keep.tile([P, P], F32)
+        make_identity(nc, identity[:])
+        ones = keep.tile([P, P], BF16)
+        nc.gpsimd.memset(ones[:], 1.0)
+        grouped = keep.tile([P, B_TILES, P, 4], BF16, align_bytes=64)
+        with tc.psum_pool(name="setup", bufs=1) as setup:
+            x_t = setup.tile([P, B_TILES, 2, P], F32)
+            for t in range(B_TILES):
+                for u in range(2):
+                    nc.tensor.transpose(
+                        x_t[:, t, u, :], x_rows[:, t, :].bitcast(F32)[:, u : K // 2 : 2], identity[:]
+                    )
+            for t in range(B_TILES):
+                nc.vector.tensor_copy(
+                    out=grouped[:, t, :, :].bitcast(F32),
+                    in_=x_t[:, t, :, :].rearrange("p u b -> p b u"),
+                )
+            nc.vector.quantize_mx(
+                out=x_words[:].bitcast(FP8X4),
+                scales=x_scales[:],
+                in_=grouped[:].rearrange("p t b j -> p (t b j)"),
+            )
+            spread_m = setup.tile([P, HM], F32)
+            nc.tensor.matmul(spread_m[:], lhsT=ones[:], rhs=slopes_row[:, 0:HM], start=True, stop=True)
+            spread_n = setup.tile([P, 32], F32)
+            nc.tensor.matmul(
+                spread_n[:], lhsT=ones[:], rhs=slopes_row[:, HM : HM + 32], start=True, stop=True
+            )
+            nc.scalar.copy(out=slope_m[:], in_=spread_m[:])
+            nc.scalar.mul(out=minus_slope_n[:], in_=spread_n[:, 0:HN], mul=-1.0)
+
+        psum = ctx.enter_context(tc.psum_pool(name="psum", bufs=4))
+
+        def project(bank, t, words, scales, cols):
+            nc.tensor.matmul_mx(
+                out=bank[:],
+                lhsT=x_words[:, t * P : (t + 1) * P].bitcast(FP8X4),
+                lhsT_scale=x_scales[:, t * P : (t + 1) * P],
+                rhs=words[:, cols].bitcast(FP8X4),
+                rhs_scale=scales[:, cols],
+                start=True,
+                stop=True,
+            )
+
+        for n in range(HN):
+            banks = []
+            lows = []
+            for t in range(B_TILES):
+                v_m = psum.tile([P, HM], F32, name="v_m")
+                project(v_m, t, im_words, im_scales, slice(n * HM, (n + 1) * HM))
+                low = work.tile([P, HM], F32, name="low")
+                nc.vector.scalar_tensor_tensor(
+                    out=low[:], in0=v_m[:], scalar=0.0, in1=slope_m[:], op0=ALU.min, op1=ALU.mult
+                )
+                banks.append(v_m)
+                lows.append(low)
+            for t in range(B_TILES):
+                nc.vector.scalar_tensor_tensor(
+                    out=total[t][:, n, :],
+                    in0=banks[t][:],
+                    scalar=0.0,
+                    in1=lows[t][:],
+                    op0=ALU.max,
+                    op1=ALU.add,
+                )
+
+        for g in range(GROUPS):
+            for t in range(B_TILES):
+                above = parts.tile([P, HN, GROUP_M], F32, name="above")
+                below = parts.tile([P, HN, GROUP_M], F32, name="below")
+                for j in range(PASSES_PER_GROUP):
+                    c = g * PASSES_PER_GROUP + j
+                    v_n = psum.tile([P, N_PASS], F32, name="v_n")
+                    project(v_n, t, in_words, in_scales, slice(c * N_PASS, (c + 1) * N_PASS))
+                    turned = v_n[:].rearrange("p (m n) -> p n m", n=HN)
+                    m_cols = slice(j * M_PER_PASS, (j + 1) * M_PER_PASS)
+                    nc.scalar.activation(out=above[:, :, m_cols], in_=turned, func=ACT.Relu)
+                    nc.scalar.activation(out=below[:, :, m_cols], in_=turned, func=ACT.Relu, scale=-1.0)
+                for n in range(HN):
+                    nc.vector.scalar_tensor_tensor(
+                        out=above[:, n, :],
+                        in0=below[:, n, :],
+                        scalar=minus_slope_n[:, n : n + 1],
+                        in1=above[:, n, :],
+                        op0=ALU.mult,
+                        op1=ALU.add,
+                    )
+                g_cols = slice(g * GROUP_M, (g + 1) * GROUP_M)
+                nc.vector.tensor_tensor(
+                    out=total[t][:, :, g_cols], in0=total[t][:, :, g_cols], in1=above[:], op=ALU.add
+                )
+                rows = slice(t * P, (t + 1) * P)
+                if g == GROUPS - 2:
+                    nc.sync.dma_start(out=out[rows, :, 0:EARLY_M], in_=total[t][:, :, 0:EARLY_M])
+                if g == GROUPS - 1:
+                    nc.sync.dma_start(out=out[rows, :, EARLY_M:HM], in_=total[t][:, :, EARLY_M:HM])

@@ -17,6 +17,7 @@ B, K, HM, HN = 256, 512, 512, 16
 B_TILES = B // P
 N_PASS = 512
 M_PER_PASS = N_PASS // HN
+M_PER_LOAD = 4
 GROUP_M = 128
 PASSES_PER_GROUP = GROUP_M // M_PER_PASS
 GROUPS = HM // GROUP_M
@@ -77,12 +78,12 @@ def tile_tensormoe_pa_e_kernel(
                 out=in_scales[row : row + 1, :].bitcast(I32).rearrange("o (m w) -> o m w", m=HM),
                 in_=W_in_scales[:, q, :].bitcast(I32).unsqueeze(0),
             )
-        for c in range(HM // M_PER_PASS):
+        for c in range(HM // M_PER_LOAD):
             nc.sync.dma_start(
-                out=in_words[:, c * N_PASS : (c + 1) * N_PASS]
+                out=in_words[:, c * M_PER_LOAD * HN : (c + 1) * M_PER_LOAD * HN]
                 .bitcast(I32)
-                .rearrange("p (m w) -> p m w", m=M_PER_PASS),
-                in_=W_in_words[c * M_PER_PASS : (c + 1) * M_PER_PASS]
+                .rearrange("p (m w) -> p m w", m=M_PER_LOAD),
+                in_=W_in_words[c * M_PER_LOAD : (c + 1) * M_PER_LOAD]
                 .rearrange("m p n t -> p m (n t)")
                 .bitcast(I32),
             )

@@ -17,7 +17,6 @@ B, K, HM, HN = 256, 512, 512, 16
 B_TILES = B // P
 N_PASS = 512
 M_PER_PASS = N_PASS // HN
-M_PER_LOAD = 4
 GROUP_M = 128
 PASSES_PER_GROUP = GROUP_M // M_PER_PASS
 GROUPS = HM // GROUP_M
@@ -72,18 +71,22 @@ def tile_tensormoe_pa_e_kernel(
                 .rearrange("g p n t -> p g (n t)")
                 .bitcast(I32),
             )
-        for q in range(16):
-            row = 32 * (q // 4) + q % 4
+        staged_scales = keep.tile([16, HM * HN], U8)
+        nc.sync.dma_start(
+            out=staged_scales[:].bitcast(I32).rearrange("q (m w) -> q m w", m=HM),
+            in_=W_in_scales.rearrange("m q n -> q m n").bitcast(I32),
+        )
+        for quad in range(4):
             nc.sync.dma_start(
-                out=in_scales[row : row + 1, :].bitcast(I32).rearrange("o (m w) -> o m w", m=HM),
-                in_=W_in_scales[:, q, :].bitcast(I32).unsqueeze(0),
+                out=in_scales[32 * quad : 32 * quad + 4, :].bitcast(I32),
+                in_=staged_scales[4 * quad : 4 * quad + 4, :].bitcast(I32),
             )
-        for c in range(HM // M_PER_LOAD):
+        for c in range(HM // M_PER_PASS):
             nc.sync.dma_start(
-                out=in_words[:, c * M_PER_LOAD * HN : (c + 1) * M_PER_LOAD * HN]
+                out=in_words[:, c * N_PASS : (c + 1) * N_PASS]
                 .bitcast(I32)
-                .rearrange("p (m w) -> p m w", m=M_PER_LOAD),
-                in_=W_in_words[c * M_PER_LOAD : (c + 1) * M_PER_LOAD]
+                .rearrange("p (m w) -> p m w", m=M_PER_PASS),
+                in_=W_in_words[c * M_PER_PASS : (c + 1) * M_PER_PASS]
                 .rearrange("m p n t -> p m (n t)")
                 .bitcast(I32),
             )

@@ -21,6 +21,7 @@ GROUP_M = 128
 PASSES_PER_GROUP = GROUP_M // M_PER_PASS
 GROUPS = HM // GROUP_M
 EARLY_M = (GROUPS - 1) * GROUP_M
+LEAD = HN - PASSES_PER_GROUP
 
 FLOPS = 2 * B * K * (HN * HM) * 2
 
@@ -30,9 +31,9 @@ def tile_tensormoe_pa_e_kernel(
 ):
     nc = tc.nc
     with ExitStack() as ctx:
+        ctx.enter_context(tc.manual_schedule())
         keep = ctx.enter_context(tc.tile_pool(name="keep", bufs=1))
         work = ctx.enter_context(tc.tile_pool(name="work", bufs=4))
-        parts = ctx.enter_context(tc.tile_pool(name="parts", bufs=3))
 
         im_words = keep.tile([P, HN * HM], U32, align_bytes=64)
         im_scales = keep.tile([P, HN * HM], U8, align_bytes=64)
@@ -44,65 +45,65 @@ def tile_tensormoe_pa_e_kernel(
         minus_slope_n = keep.tile([P, HN], F32)
         total = [keep.tile([P, HN, HM], F32, name="total%d" % t) for t in range(B_TILES)]
 
-        nc.vector.memset(im_scales[:].bitcast(I32), 0)
-        nc.vector.memset(in_scales[:].bitcast(I32), 0)
+        with tc.tile_pool(name="early", bufs=1) as early, tc.psum_pool(name="setup", bufs=1) as setup:
+            nc.vector.memset(im_scales[:].bitcast(I32), 0)
+            nc.vector.memset(in_scales[:].bitcast(I32), 0)
+            identity = early.tile([P, P], F32)
+            make_identity(nc, identity[:])
+            slopes_row = early.tile([P, HM + 32], BF16)
+            nc.gpsimd.memset(slopes_row[:], 0.0)
+            ones = early.tile([P, P], BF16)
+            nc.gpsimd.memset(ones[:], 1.0)
 
-        x_rows = keep.tile([P, B_TILES, K], BF16)
-        nc.sync.dma_start(out=x_rows[:], in_=x.rearrange("(t b) k -> b t k", b=P))
-        for quad in range(4):
+            x_rows = early.tile([P, B_TILES, K], BF16)
+            nc.sync.dma_start(out=x_rows[:], in_=x.rearrange("(t b) k -> b t k", b=P))
+            for quad in range(4):
+                nc.sync.dma_start(
+                    out=im_scales[32 * quad : 32 * quad + 4, :]
+                    .bitcast(I32)
+                    .rearrange("r (g w) -> r g w", g=HN),
+                    in_=W_im_scales[:, 4 * quad : 4 * quad + 4, :]
+                    .rearrange("g r c -> r g c")
+                    .bitcast(I32),
+                )
+            nc.sync.dma_start(out=slopes_row[0:1, 0:HM], in_=leak_m.unsqueeze(0))
+            nc.sync.dma_start(out=slopes_row[0:1, HM : HM + HN], in_=leak_n.unsqueeze(0))
+            for j in range(4):
+                nc.sync.dma_start(
+                    out=im_words[:, 4 * j * HM : 4 * (j + 1) * HM]
+                    .bitcast(I32)
+                    .rearrange("p (g w) -> p g w", g=4),
+                    in_=W_im_words[4 * j : 4 * (j + 1)]
+                    .rearrange("g p n t -> p g (n t)")
+                    .bitcast(I32),
+                )
+            staged_scales = early.tile([16, HM * HN], U8)
             nc.sync.dma_start(
-                out=im_scales[32 * quad : 32 * quad + 4, :]
-                .bitcast(I32)
-                .rearrange("r (g w) -> r g w", g=HN),
-                in_=W_im_scales[:, 4 * quad : 4 * quad + 4, :]
-                .rearrange("g r c -> r g c")
-                .bitcast(I32),
+                out=staged_scales[:].bitcast(I32).rearrange("q (m w) -> q m w", m=HM),
+                in_=W_in_scales.rearrange("m q n -> q m n").bitcast(I32),
             )
-        slopes_row = keep.tile([P, HM + 32], BF16)
-        nc.gpsimd.memset(slopes_row[:], 0.0)
-        nc.sync.dma_start(out=slopes_row[0:1, 0:HM], in_=leak_m.unsqueeze(0))
-        nc.sync.dma_start(out=slopes_row[0:1, HM : HM + HN], in_=leak_n.unsqueeze(0))
-        for j in range(4):
-            nc.sync.dma_start(
-                out=im_words[:, 4 * j * HM : 4 * (j + 1) * HM]
-                .bitcast(I32)
-                .rearrange("p (g w) -> p g w", g=4),
-                in_=W_im_words[4 * j : 4 * (j + 1)]
-                .rearrange("g p n t -> p g (n t)")
-                .bitcast(I32),
-            )
-        staged_scales = keep.tile([16, HM * HN], U8)
-        nc.sync.dma_start(
-            out=staged_scales[:].bitcast(I32).rearrange("q (m w) -> q m w", m=HM),
-            in_=W_in_scales.rearrange("m q n -> q m n").bitcast(I32),
-        )
-        for quad in range(4):
-            nc.sync.dma_start(
-                out=in_scales[32 * quad : 32 * quad + 4, :].bitcast(I32),
-                in_=staged_scales[4 * quad : 4 * quad + 4, :].bitcast(I32),
-            )
-        for c in range(HM // M_PER_PASS):
-            nc.sync.dma_start(
-                out=in_words[:, c * N_PASS : (c + 1) * N_PASS]
-                .bitcast(I32)
-                .rearrange("p (m w) -> p m w", m=M_PER_PASS),
-                in_=W_in_words[c * M_PER_PASS : (c + 1) * M_PER_PASS]
-                .rearrange("m p n t -> p m (n t)")
-                .bitcast(I32),
-            )
+            for quad in range(4):
+                nc.sync.dma_start(
+                    out=in_scales[32 * quad : 32 * quad + 4, :].bitcast(I32),
+                    in_=staged_scales[4 * quad : 4 * quad + 4, :].bitcast(I32),
+                )
+            for c in range(HM // M_PER_PASS):
+                nc.sync.dma_start(
+                    out=in_words[:, c * N_PASS : (c + 1) * N_PASS]
+                    .bitcast(I32)
+                    .rearrange("p (m w) -> p m w", m=M_PER_PASS),
+                    in_=W_in_words[c * M_PER_PASS : (c + 1) * M_PER_PASS]
+                    .rearrange("m p n t -> p m (n t)")
+                    .bitcast(I32),
+                )
 
-        identity = keep.tile([P, P], F32)
-        make_identity(nc, identity[:])
-        ones = keep.tile([P, P], BF16)
-        nc.gpsimd.memset(ones[:], 1.0)
-        grouped = keep.tile([P, B_TILES, P, 4], BF16, align_bytes=64)
-        with tc.psum_pool(name="setup", bufs=1) as setup:
             x_t = setup.tile([P, B_TILES, 2, P], F32)
             for t in range(B_TILES):
                 for u in range(2):
                     nc.tensor.transpose(
                         x_t[:, t, u, :], x_rows[:, t, :].bitcast(F32)[:, u : K // 2 : 2], identity[:]
                     )
+            grouped = early.tile([P, B_TILES, P, 4], BF16, align_bytes=64)
             for t in range(B_TILES):
                 nc.vector.tensor_copy(
                     out=grouped[:, t, :, :].bitcast(F32),
@@ -122,6 +123,7 @@ def tile_tensormoe_pa_e_kernel(
             nc.scalar.copy(out=slope_m[:], in_=spread_m[:])
             nc.scalar.mul(out=minus_slope_n[:], in_=spread_n[:, 0:HN], mul=-1.0)
 
+        parts = ctx.enter_context(tc.tile_pool(name="parts", bufs=4))
         psum = ctx.enter_context(tc.psum_pool(name="psum", bufs=4))
 
         def project(bank, t, words, scales, cols):
@@ -135,7 +137,7 @@ def tile_tensormoe_pa_e_kernel(
                 stop=True,
             )
 
-        for n in range(HN):
+        def project_im(n):
             banks = []
             lows = []
             for t in range(B_TILES):
@@ -157,33 +159,61 @@ def tile_tensormoe_pa_e_kernel(
                     op1=ALU.add,
                 )
 
-        for g in range(GROUPS):
+        def project_in(g, j, above, below):
+            c = g * PASSES_PER_GROUP + j
+            m_cols = slice(j * M_PER_PASS, (j + 1) * M_PER_PASS)
             for t in range(B_TILES):
-                above = parts.tile([P, HN, GROUP_M], F32, name="above")
-                below = parts.tile([P, HN, GROUP_M], F32, name="below")
-                for j in range(PASSES_PER_GROUP):
-                    c = g * PASSES_PER_GROUP + j
-                    v_n = psum.tile([P, N_PASS], F32, name="v_n")
-                    project(v_n, t, in_words, in_scales, slice(c * N_PASS, (c + 1) * N_PASS))
-                    turned = v_n[:].rearrange("p (m n) -> p n m", n=HN)
-                    m_cols = slice(j * M_PER_PASS, (j + 1) * M_PER_PASS)
-                    nc.scalar.activation(out=above[:, :, m_cols], in_=turned, func=ACT.Relu)
-                    nc.scalar.activation(out=below[:, :, m_cols], in_=turned, func=ACT.Relu, scale=-1.0)
+                v_n = psum.tile([P, N_PASS], F32, name="v_n")
+                project(v_n, t, in_words, in_scales, slice(c * N_PASS, (c + 1) * N_PASS))
+                v_runs = v_n[:].rearrange("p (m a k) -> p a m k", a=4, k=4)
+                nc.scalar.activation(
+                    out=above[t][:, :, m_cols].rearrange("p (a k) m -> p a m k", k=4),
+                    in_=v_runs,
+                    func=ACT.Relu,
+                )
+                nc.scalar.activation(
+                    out=below[t][:, :, m_cols].rearrange("p (a k) m -> p a m k", k=4),
+                    in_=v_runs,
+                    func=ACT.Relu,
+                    scale=-1.0,
+                )
+
+        def join(g, above, below):
+            g_cols = slice(g * GROUP_M, (g + 1) * GROUP_M)
+            for t in range(B_TILES):
                 for n in range(HN):
                     nc.vector.scalar_tensor_tensor(
-                        out=above[:, n, :],
-                        in0=below[:, n, :],
+                        out=above[t][:, n, :],
+                        in0=below[t][:, n, :],
                         scalar=minus_slope_n[:, n : n + 1],
-                        in1=above[:, n, :],
+                        in1=above[t][:, n, :],
                         op0=ALU.mult,
                         op1=ALU.add,
                     )
-                g_cols = slice(g * GROUP_M, (g + 1) * GROUP_M)
                 nc.vector.tensor_tensor(
-                    out=total[t][:, :, g_cols], in0=total[t][:, :, g_cols], in1=above[:], op=ALU.add
+                    out=total[t][:, :, g_cols], in0=total[t][:, :, g_cols], in1=above[t][:], op=ALU.add
                 )
                 rows = slice(t * P, (t + 1) * P)
                 if g == GROUPS - 2:
                     nc.sync.dma_start(out=out[rows, :, 0:EARLY_M], in_=total[t][:, :, 0:EARLY_M])
                 if g == GROUPS - 1:
                     nc.sync.dma_start(out=out[rows, :, EARLY_M:HM], in_=total[t][:, :, EARLY_M:HM])
+
+        def new_parts():
+            above = [parts.tile([P, HN, GROUP_M], F32, name="above") for t in range(B_TILES)]
+            below = [parts.tile([P, HN, GROUP_M], F32, name="below") for t in range(B_TILES)]
+            return above, below
+
+        for n in range(LEAD):
+            project_im(n)
+        split = new_parts()
+        for j in range(PASSES_PER_GROUP):
+            project_in(0, j, split[0], split[1])
+            project_im(LEAD + j)
+        for g in range(1, GROUPS):
+            earlier = split
+            split = new_parts()
+            for j in range(PASSES_PER_GROUP):
+                project_in(g, j, split[0], split[1])
+            join(g - 1, earlier[0], earlier[1])
+        join(GROUPS - 1, split[0], split[1])

@@ -22,6 +22,8 @@ PASSES_PER_GROUP = GROUP_M // M_PER_PASS
 GROUPS = HM // GROUP_M
 EARLY_M = (GROUPS - 1) * GROUP_M
 LEAD = HN - PASSES_PER_GROUP
+IN_LOADS = HM // M_PER_PASS
+SCALAR_LOADS = 4
 
 FLOPS = 2 * B * K * (HN * HM) * 2
 
@@ -77,25 +79,34 @@ def tile_tensormoe_pa_e_kernel(
                     .rearrange("g p n t -> p g (n t)")
                     .bitcast(I32),
                 )
+
+            def load_in_words(queue, view, c):
+                queue.dma_start(
+                    out=in_words[:, c * N_PASS : (c + 1) * N_PASS]
+                    .bitcast(view)
+                    .rearrange("p (m w) -> p m w", m=M_PER_PASS),
+                    in_=W_in_words[c * M_PER_PASS : (c + 1) * M_PER_PASS]
+                    .rearrange("m p n t -> p m (n t)")
+                    .bitcast(view),
+                )
+
             staged_scales = early.tile([16, HM * HN], U8)
-            nc.sync.dma_start(
-                out=staged_scales[:].bitcast(I32).rearrange("q (m w) -> q m w", m=HM),
-                in_=W_in_scales.rearrange("m q n -> q m n").bitcast(I32),
+            nc.scalar.dma_start(
+                out=staged_scales[:].bitcast(F32).rearrange("q (m w) -> q m w", m=HM),
+                in_=W_in_scales.rearrange("m q n -> q m n").bitcast(F32),
             )
+            for c in range(3):
+                load_in_words(nc.sync, I32, c)
+            load_in_words(nc.scalar, F32, IN_LOADS - SCALAR_LOADS)
             for quad in range(4):
                 nc.sync.dma_start(
                     out=in_scales[32 * quad : 32 * quad + 4, :].bitcast(I32),
                     in_=staged_scales[4 * quad : 4 * quad + 4, :].bitcast(I32),
                 )
-            for c in range(HM // M_PER_PASS):
-                nc.sync.dma_start(
-                    out=in_words[:, c * N_PASS : (c + 1) * N_PASS]
-                    .bitcast(I32)
-                    .rearrange("p (m w) -> p m w", m=M_PER_PASS),
-                    in_=W_in_words[c * M_PER_PASS : (c + 1) * M_PER_PASS]
-                    .rearrange("m p n t -> p m (n t)")
-                    .bitcast(I32),
-                )
+            for c in range(IN_LOADS - SCALAR_LOADS + 1, IN_LOADS):
+                load_in_words(nc.scalar, F32, c)
+            for c in range(3, IN_LOADS - SCALAR_LOADS):
+                load_in_words(nc.sync, I32, c)
 
             x_t = setup.tile([P, B_TILES, 2, P], F32)
             for t in range(B_TILES):
@@ -120,8 +131,8 @@ def tile_tensormoe_pa_e_kernel(
             nc.tensor.matmul(
                 spread_n[:], lhsT=ones[:], rhs=slopes_row[:, HM : HM + 32], start=True, stop=True
             )
-            nc.scalar.copy(out=slope_m[:], in_=spread_m[:])
-            nc.scalar.mul(out=minus_slope_n[:], in_=spread_n[:, 0:HN], mul=-1.0)
+            nc.vector.tensor_copy(out=slope_m[:], in_=spread_m[:])
+            nc.vector.tensor_scalar_mul(out=minus_slope_n[:], in0=spread_n[:, 0:HN], scalar1=-1.0)
 
         parts = ctx.enter_context(tc.tile_pool(name="parts", bufs=4))
         psum = ctx.enter_context(tc.psum_pool(name="psum", bufs=4))

from contextlib import ExitStack

import concourse.mybir as mybir
from concourse.masks import make_identity

F32 = mybir.dt.float32
BF16 = mybir.dt.bfloat16
I32 = mybir.dt.int32
U32 = mybir.dt.uint32
U8 = mybir.dt.uint8
FP8X4 = mybir.dt.float8_e4m3fn_x4
ALU = mybir.AluOpType
ACT = mybir.ActivationFunctionType

P = 128
B, K, HM, HN = 256, 512, 512, 16
B_TILES = B // P
N_PASS = 512
M_PER_PASS = N_PASS // HN
GROUP_M = 128
PASSES_PER_GROUP = GROUP_M // M_PER_PASS
GROUPS = HM // GROUP_M
EARLY_M = (GROUPS - 1) * GROUP_M
LEAD = HN - PASSES_PER_GROUP
IN_LOADS = HM // M_PER_PASS
SCALAR_LOADS = 4

FLOPS = 2 * B * K * (HN * HM) * 2


def tile_tensormoe_pa_e_kernel(
    tc, x, W_im_words, W_im_scales, W_in_words, W_in_scales, leak_m, leak_n, out
):
    nc = tc.nc
    with ExitStack() as ctx:
        ctx.enter_context(tc.manual_schedule())
        keep = ctx.enter_context(tc.tile_pool(name="keep", bufs=1))
        work = ctx.enter_context(tc.tile_pool(name="work", bufs=4))

        im_words = keep.tile([P, HN * HM], U32, align_bytes=64)
        im_scales = keep.tile([P, HN * HM], U8, align_bytes=64)
        in_words = keep.tile([P, HM * HN], U32, align_bytes=64)
        in_scales = keep.tile([P, HM * HN], U8, align_bytes=64)
        x_words = keep.tile([P, B], U32, align_bytes=64)
        x_scales = keep.tile([P, B], U8, align_bytes=64)
        slope_m = keep.tile([P, HM], F32)
        minus_slope_n = keep.tile([P, HN], F32)
        total = [keep.tile([P, HN, HM], F32, name="total%d" % t) for t in range(B_TILES)]

        with tc.tile_pool(name="early", bufs=1) as early, tc.psum_pool(name="setup", bufs=1) as setup:
            nc.vector.memset(im_scales[:].bitcast(I32), 0)
            nc.vector.memset(in_scales[:].bitcast(I32), 0)
            identity = early.tile([P, P], F32)
            make_identity(nc, identity[:])
            slopes_row = early.tile([P, HM + 32], BF16)
            nc.gpsimd.memset(slopes_row[:], 0.0)
            ones = early.tile([P, P], BF16)
            nc.gpsimd.memset(ones[:], 1.0)

            x_rows = early.tile([P, B_TILES, K], BF16)
            nc.sync.dma_start(out=x_rows[:], in_=x.rearrange("(t b) k -> b t k", b=P))
            for quad in range(4):
                nc.sync.dma_start(
                    out=im_scales[32 * quad : 32 * quad + 4, :]
                    .bitcast(I32)
                    .rearrange("r (g w) -> r g w", g=HN),
                    in_=W_im_scales[:, 4 * quad : 4 * quad + 4, :]
                    .rearrange("g r c -> r g c")
                    .bitcast(I32),
                )
            nc.sync.dma_start(out=slopes_row[0:1, 0:HM], in_=leak_m.unsqueeze(0))
            nc.sync.dma_start(out=slopes_row[0:1, HM : HM + HN], in_=leak_n.unsqueeze(0))
            for j in range(4):
                nc.sync.dma_start(
                    out=im_words[:, 4 * j * HM : 4 * (j + 1) * HM]
                    .bitcast(I32)
                    .rearrange("p (g w) -> p g w", g=4),
                    in_=W_im_words[4 * j : 4 * (j + 1)]
                    .rearrange("g p n t -> p g (n t)")
                    .bitcast(I32),
                )

            def load_in_words(queue, view, c):
                queue.dma_start(
                    out=in_words[:, c * N_PASS : (c + 1) * N_PASS]
                    .bitcast(view)
                    .rearrange("p (m w) -> p m w", m=M_PER_PASS),
                    in_=W_in_words[c * M_PER_PASS : (c + 1) * M_PER_PASS]
                    .rearrange("m p n t -> p m (n t)")
                    .bitcast(view),
                )

            staged_scales = early.tile([16, HM * HN], U8)
            nc.scalar.dma_start(
                out=staged_scales[:].bitcast(F32).rearrange("q (m w) -> q m w", m=HM),
                in_=W_in_scales.rearrange("m q n -> q m n").bitcast(F32),
            )
            for c in range(3):
                load_in_words(nc.sync, I32, c)
            load_in_words(nc.scalar, F32, IN_LOADS - SCALAR_LOADS)
            for quad in range(4):
                nc.sync.dma_start(
                    out=in_scales[32 * quad : 32 * quad + 4, :].bitcast(I32),
                    in_=staged_scales[4 * quad : 4 * quad + 4, :].bitcast(I32),
                )
            for c in range(IN_LOADS - SCALAR_LOADS + 1, IN_LOADS):
                load_in_words(nc.scalar, F32, c)
            for c in range(3, IN_LOADS - SCALAR_LOADS):
                load_in_words(nc.sync, I32, c)

            x_t = setup.tile([P, B_TILES, 2, P], F32)
            for t in range(B_TILES):
                for u in range(2):
                    nc.tensor.transpose(
                        x_t[:, t, u, :], x_rows[:, t, :].bitcast(F32)[:, u : K // 2 : 2], identity[:]
                    )
            grouped = early.tile([P, B_TILES, P, 4], BF16, align_bytes=64)
            for t in range(B_TILES):
                nc.vector.tensor_copy(
                    out=grouped[:, t, :, :].bitcast(F32),
                    in_=x_t[:, t, :, :].rearrange("p u b -> p b u"),
                )
            nc.vector.quantize_mx(
                out=x_words[:].bitcast(FP8X4),
                scales=x_scales[:],
                in_=grouped[:].rearrange("p t b j -> p (t b j)"),
            )
            spread_m = setup.tile([P, HM], F32)
            nc.tensor.matmul(spread_m[:], lhsT=ones[:], rhs=slopes_row[:, 0:HM], start=True, stop=True)
            spread_n = setup.tile([P, 32], F32)
            nc.tensor.matmul(
                spread_n[:], lhsT=ones[:], rhs=slopes_row[:, HM : HM + 32], start=True, stop=True
            )
            nc.vector.tensor_copy(out=slope_m[:], in_=spread_m[:])
            nc.vector.tensor_scalar_mul(out=minus_slope_n[:], in0=spread_n[:, 0:HN], scalar1=-1.0)

        parts = ctx.enter_context(tc.tile_pool(name="parts", bufs=4))
        psum = ctx.enter_context(tc.psum_pool(name="psum", bufs=4))

        def project(bank, t, words, scales, cols):
            nc.tensor.matmul_mx(
                out=bank[:],
                lhsT=x_words[:, t * P : (t + 1) * P].bitcast(FP8X4),
                lhsT_scale=x_scales[:, t * P : (t + 1) * P],
                rhs=words[:, cols].bitcast(FP8X4),
                rhs_scale=scales[:, cols],
                start=True,
                stop=True,
            )

        def project_im(n):
            banks = []
            lows = []
            for t in range(B_TILES):
                v_m = psum.tile([P, HM], F32, name="v_m")
                project(v_m, t, im_words, im_scales, slice(n * HM, (n + 1) * HM))
                low = work.tile([P, HM], F32, name="low")
                nc.vector.scalar_tensor_tensor(
                    out=low[:], in0=v_m[:], scalar=0.0, in1=slope_m[:], op0=ALU.min, op1=ALU.mult
                )
                banks.append(v_m)
                lows.append(low)
            for t in range(B_TILES):
                nc.vector.scalar_tensor_tensor(
                    out=total[t][:, n, :],
                    in0=banks[t][:],
                    scalar=0.0,
                    in1=lows[t][:],
                    op0=ALU.max,
                    op1=ALU.add,
                )

        def project_in(g, j, above, below):
            c = g * PASSES_PER_GROUP + j
            m_cols = slice(j * M_PER_PASS, (j + 1) * M_PER_PASS)
            for t in range(B_TILES):
                v_n = psum.tile([P, N_PASS], F32, name="v_n")
                project(v_n, t, in_words, in_scales, slice(c * N_PASS, (c + 1) * N_PASS))
                v_runs = v_n[:].rearrange("p (m a k) -> p a m k", a=4, k=4)
                nc.scalar.activation(
                    out=above[t][:, :, m_cols].rearrange("p (a k) m -> p a m k", k=4),
                    in_=v_runs,
                    func=ACT.Relu,
                )
                nc.scalar.activation(
                    out=below[t][:, :, m_cols].rearrange("p (a k) m -> p a m k", k=4),
                    in_=v_runs,
                    func=ACT.Relu,
                    scale=-1.0,
                )

        def join(g, above, below):
            g_cols = slice(g * GROUP_M, (g + 1) * GROUP_M)
            for t in range(B_TILES):
                for n in range(HN):
                    nc.vector.scalar_tensor_tensor(
                        out=above[t][:, n, :],
                        in0=below[t][:, n, :],
                        scalar=minus_slope_n[:, n : n + 1],
                        in1=above[t][:, n, :],
                        op0=ALU.mult,
                        op1=ALU.add,
                    )
                nc.vector.tensor_tensor(
                    out=total[t][:, :, g_cols], in0=total[t][:, :, g_cols], in1=above[t][:], op=ALU.add
                )
                rows = slice(t * P, (t + 1) * P)
                if g == GROUPS - 2:
                    nc.sync.dma_start(out=out[rows, :, 0:EARLY_M], in_=total[t][:, :, 0:EARLY_M])
                if g == GROUPS - 1:
                    nc.sync.dma_start(out=out[rows, :, EARLY_M:HM], in_=total[t][:, :, EARLY_M:HM])

        def new_parts():
            above = [parts.tile([P, HN, GROUP_M], F32, name="above") for t in range(B_TILES)]
            below = [parts.tile([P, HN, GROUP_M], F32, name="below") for t in range(B_TILES)]
            return above, below

        for n in range(LEAD):
            project_im(n)
        split = new_parts()
        for j in range(PASSES_PER_GROUP):
            project_in(0, j, split[0], split[1])
            project_im(LEAD + j)
        for g in range(1, GROUPS):
            earlier = split
            split = new_parts()
            for j in range(PASSES_PER_GROUP):
                project_in(g, j, split[0], split[1])
            join(g - 1, earlier[0], earlier[1])
        join(GROUPS - 1, split[0], split[1])
